import numpy as np
import ml_dtypes


def mxq(x, axis, fmt="e4m3"):
    dtype, down = {"e4m3": (ml_dtypes.float8_e4m3fn, 7), "e5m2": (ml_dtypes.float8_e5m2, 14)}[fmt]
    v = np.moveaxis(np.asarray(x, np.float32).astype(ml_dtypes.bfloat16).astype(np.float64), axis, -1)
    blocks = v.reshape(v.shape[:-1] + (-1, 32))
    amax = np.abs(blocks).max(-1, keepdims=True)
    byte = np.maximum(np.where(amax > 0, np.frexp(amax)[1] - 1 + 127, 0) - down, 1)
    scale = np.exp2(byte - 127.0)
    codes = (blocks / scale).astype(np.float32).astype(dtype).astype(np.float64)
    return np.moveaxis((codes * scale).reshape(v.shape), -1, axis)


WIDE = False


def mx_kscale(k):
    if not WIDE:
        return np.ones(k)
    levels = np.array([10, -10, 5, -5, 0])
    a = np.random.permutation(np.resize(levels, k // 512 * 4)).reshape(k // 512, 4)
    idx = np.arange(k)
    return np.exp2(a[idx // 512, idx % 128 // 32])


BF16 = ml_dtypes.bfloat16


def bf(x):
    return np.asarray(x, np.float32).astype(BF16)


def f64(x):
    return np.asarray(x).astype(np.float64)


B, H, W, C, D, P = 128, 4, 7, 512, 256, 128
F = H * W * D
STRIDE = 16.0


def safe_exp(v):
    return np.exp(np.clip(v, -10.0, 10.0))


def setup_inputs():
    s = mx_kscale(C)
    t = mx_kscale(F)[:D]
    tf = np.tile(t, H * W)[:, None]
    return {"features": bf(np.random.standard_normal((B, H, W, C)) * s),
            "roi": bf(np.random.uniform(0.02, 0.125, (B, P, 4))),
            "conv_w": bf(np.random.standard_normal((C, D)) / np.sqrt(C) / s[:, None] * t),
            "conv_b": bf(np.random.standard_normal(D) * 0.2 * t),
            "cls_w": bf(np.random.standard_normal((F, 2 * P)) * 1.5 / np.sqrt(F) / tf),
            "cls_b": bf(np.random.standard_normal(2 * P) * 0.5),
            "bbox_w": bf(np.random.standard_normal((F, 4 * P)) * 0.7 / np.sqrt(F) / tf),
            "bbox_b": bf(np.random.standard_normal(4 * P) * 0.3)}


def reference(features, roi, conv_w, conv_b, cls_w, cls_b, bbox_w, bbox_b):
    h = np.maximum((mxq(f64(features).reshape(B * H * W, C), 1, "e4m3") @ mxq(f64(conv_w), 0, "e4m3")) + f64(conv_b), 0.0)
    flatq = mxq(h.reshape(B, F), 1, "e4m3")
    cls = (flatq @ mxq(f64(cls_w), 0, "e4m3")) + f64(cls_b)
    bbox = (flatq @ mxq(f64(bbox_w)[:, P:], 0, "e4m3")) + f64(bbox_b)[P:]
    obj = np.stack([cls[:, :P], cls[:, P:]], axis=0)
    e = np.exp(obj - obj.max(axis=0, keepdims=True))
    objectness = (e / e.sum(axis=0, keepdims=True))[1]
    roi_img = f64(roi) * STRIDE
    bb = np.transpose(bbox.reshape(B, 3, P), (0, 2, 1))
    x = roi_img[:, :, 0] - bb[:, :, 0] * roi_img[:, :, 3]
    y = roi_img[:, :, 1]
    w = roi_img[:, :, 2] * safe_exp(bb[:, :, 1])
    hh = roi_img[:, :, 3] * safe_exp(bb[:, :, 2])
    return np.stack([x, y, w, hh, objectness], axis=-1)

@@ -1,0 +1,290 @@
+from contextlib import ExitStack
+
+import concourse.mybir as mybir
+from concourse.masks import make_identity
+
+F32 = mybir.dt.float32
+BF16 = mybir.dt.bfloat16
+U32 = mybir.dt.uint32
+U8 = mybir.dt.uint8
+FP8X4 = mybir.dt.float8_e4m3fn_x4
+ACT = mybir.ActivationFunctionType
+ALU = mybir.AluOpType
+
+P = 128
+PACK = 4
+POSITIONS = 28
+CHANNELS = 512
+HIDDEN = 256
+CHUNKS = POSITIONS // PACK
+HALVES = HIDDEN // P
+CLS_COLS = 256
+BOX_COLS = 384
+HEAD_COLS = CLS_COLS + BOX_COLS
+WIDE = 512
+STRIDE = 16.0
+
+FLOPS = 2 * P * POSITIONS * CHANNELS * HIDDEN + 2 * P * POSITIONS * HIDDEN * HEAD_COLS
+BYTES = (
+    2 * (P * POSITIONS * CHANNELS + P * P * 4 + CHANNELS * HIDDEN + HIDDEN)
+    + 2 * (POSITIONS * HIDDEN + 1) * HEAD_COLS
+    + 4 * P * P * 5
+)
+
+
+def tile_classifiermodel_kernel(
+    tc, features, roi, conv_w, conv_b, cls_w, cls_b, bbox_w, bbox_b, out
+):
+    nc = tc.nc
+    with ExitStack() as ctx:
+        const = ctx.enter_context(tc.tile_pool(name="const", bufs=1))
+        raw = ctx.enter_context(tc.tile_pool(name="raw", bufs=CHUNKS))
+        stage = ctx.enter_context(tc.tile_pool(name="stage", bufs=3))
+        wstage = ctx.enter_context(tc.tile_pool(name="wstage", bufs=4))
+        psum_t = ctx.enter_context(tc.psum_pool(name="psum_t", bufs=4))
+        psum_h = ctx.enter_context(tc.psum_pool(name="psum_h", bufs=2))
+        psum_acc = ctx.enter_context(tc.psum_pool(name="psum_acc", bufs=1))
+
+        cw_raw = const.tile([P, PACK, HIDDEN], BF16)
+        nc.sync.dma_start(
+            out=cw_raw[:].rearrange("q (u f) n -> q u f n", u=2),
+            in_=conv_w.rearrange("(u q f) n -> q u f n", u=2, f=2),
+        )
+
+        feat_rows = features.rearrange("b h w c -> b (h w) c")
+        feat_raw = []
+        cls_raw = []
+        box_raw = []
+
+        def load_features(g):
+            tile_f = raw.tile([P, PACK, CHANNELS], BF16, name="feat_raw")
+            nc.sync.dma_start(out=tile_f[:], in_=feat_rows[:, PACK * g : PACK * (g + 1), :])
+            feat_raw.append(tile_f)
+
+        def load_weights(g):
+            rows = slice(PACK * HIDDEN * g, PACK * HIDDEN * (g + 1))
+            tile_c = raw.tile([P, PACK, HALVES, CLS_COLS], BF16, name="cls_raw")
+            nc.sync.dma_start(
+                out=tile_c[:],
+                in_=cls_w[rows, :].rearrange("(t q e) n -> q t e n", t=PACK, e=HALVES),
+            )
+            cls_raw.append(tile_c)
+            tile_b = raw.tile([P, HALVES, PACK, BOX_COLS], BF16, name="box_raw")
+            box_rows = bbox_w[rows, P:].rearrange("(t q e) n -> q e t n", t=PACK, e=HALVES)
+            for e in range(HALVES):
+                nc.sync.dma_start(out=tile_b[:, e], in_=box_rows[:, e])
+            box_raw.append(tile_b)
+
+        load_features(0)
+        load_features(1)
+        for g in range(CHUNKS):
+            if g + 2 < CHUNKS:
+                load_features(g + 2)
+            load_weights(g)
+
+        convb_bf = const.tile([P, HALVES], BF16)
+        nc.scalar.dma_start(out=convb_bf[:], in_=conv_b.rearrange("(q e) -> q e", e=HALVES))
+        roi_raw = const.tile([P, P, 4], BF16)
+        nc.scalar.dma_start(out=roi_raw[:], in_=roi)
+        bias_rows = const.tile([P, HEAD_COLS], BF16)
+        nc.vector.memset(bias_rows[:], 0.0)
+        nc.scalar.dma_start(out=bias_rows[0:1, 0:CLS_COLS], in_=cls_b.unsqueeze(0))
+        nc.scalar.dma_start(out=bias_rows[0:1, CLS_COLS:HEAD_COLS], in_=bbox_b[P:].unsqueeze(0))
+
+        warm = const.tile([P, 1], F32)
+        nc.vector.memset(warm[:], 0.0)
+        nc.scalar.activation(out=warm[:], in_=warm[:], func=ACT.Exp)
+
+        ident = const.tile([P, P], F32)
+        make_identity(nc, ident[:])
+        ones = const.tile([P, P], BF16)
+        nc.vector.memset(ones[:], 1.0)
+
+        convb = const.tile([P, HALVES], F32)
+        nc.vector.tensor_copy(out=convb[:], in_=convb_bf[:])
+
+        cw_grouped = const.tile([P, HIDDEN, PACK], BF16, align_bytes=64)
+        for e in range(HALVES):
+            nc.vector.tensor_copy(
+                out=cw_grouped[:, P * e : P * (e + 1), :],
+                in_=cw_raw[:].rearrange("q k (m e) -> q e m k", e=HALVES)[:, e],
+            )
+        cw_codes = const.tile([P, HIDDEN], U32, align_bytes=64)
+        cw_scales = const.tile([P, HIDDEN], U8, align_bytes=64)
+        nc.vector.quantize_mx(
+            out=cw_codes[:].bitcast(FP8X4),
+            scales=cw_scales[:],
+            in_=cw_grouped[:].rearrange("q n k -> q (n k)"),
+        )
+
+        bias_all = const.tile([P, HEAD_COLS], F32)
+        for lo, hi in ((0, WIDE), (WIDE, HEAD_COLS)):
+            spread = psum_h.tile([P, WIDE], F32, name="hidden_ps")
+            nc.tensor.matmul(
+                out=spread[:, 0 : hi - lo], lhsT=ones[:], rhs=bias_rows[:, lo:hi], start=True, stop=True
+            )
+            nc.vector.tensor_copy(out=bias_all[:, lo:hi], in_=spread[:, 0 : hi - lo])
+
+        r = const.tile([P, 4, P], F32)
+        nc.vector.tensor_scalar(
+            out=r[:],
+            in0=roi_raw[:].rearrange("b n c -> b c n"),
+            scalar1=STRIDE,
+            scalar2=None,
+            op0=ALU.mult,
+        )
+
+        acc_wide = psum_acc.tile([P, WIDE], F32)
+        acc_rest = psum_acc.tile([P, HEAD_COLS - WIDE], F32)
+
+        feat_grouped = {}
+        feat_codes = {}
+        hid_grouped = {}
+        hid_codes = {}
+        w_grouped = {}
+
+        def transpose_features(g):
+            words = feat_raw[g][:].bitcast(F32)
+            grouped = stage.tile([P, PACK * P, PACK], BF16, name="feat_grouped", align_bytes=64)
+            grouped_words = grouped[:].bitcast(F32)
+            for pair in range(2):
+                bank = psum_t.tile([P, 2, 2, P], F32, name="feat_t")
+                for t in range(2):
+                    for u in range(2):
+                        nc.tensor.transpose(
+                            bank[:, t, u, :], words[:, 2 * pair + t, P * u : P * (u + 1)], ident[:]
+                        )
+                nc.scalar.copy(
+                    out=grouped_words[:, 2 * P * pair : 2 * P * (pair + 1), :].rearrange(
+                        "q (t b) u -> q t b u", t=2
+                    ),
+                    in_=bank[:].rearrange("q t u b -> q t b u"),
+                )
+            feat_grouped[g] = grouped
+
+        def quantise_features(g):
+            codes = stage.tile([P, PACK * P], U32, name="feat_codes", align_bytes=64)
+            scales = stage.tile([P, PACK * P], U8, name="feat_scales", align_bytes=64)
+            nc.vector.quantize_mx(
+                out=codes[:].bitcast(FP8X4),
+                scales=scales[:],
+                in_=feat_grouped[g][:].rearrange("q c k -> q (c k)"),
+            )
+            feat_codes[g] = (codes, scales)
+
+        def convolve(g):
+            codes, scales = feat_codes[g]
+            grouped = stage.tile([P, HALVES, P, PACK], BF16, name="hid_grouped", align_bytes=64)
+            for e in range(HALVES):
+                hidden_ps = psum_h.tile([P, WIDE], F32, name="hidden_ps")
+                nc.tensor.matmul_mx(
+                    out=hidden_ps[:],
+                    lhsT=cw_codes[:, P * e : P * (e + 1)].bitcast(FP8X4),
+                    lhsT_scale=cw_scales[:, P * e : P * (e + 1)],
+                    rhs=codes[:].bitcast(FP8X4),
+                    rhs_scale=scales[:],
+                    start=True,
+                    stop=True,
+                )
+                nc.scalar.activation(
+                    out=grouped[:, e],
+                    in_=hidden_ps[:].rearrange("q (t b) -> q b t", t=PACK),
+                    func=ACT.Relu,
+                    bias=convb[:, e : e + 1],
+                )
+            hid_grouped[g] = grouped
+
+        def quantise_hidden(g):
+            codes = stage.tile([P, HALVES, P], U32, name="hid_codes", align_bytes=64)
+            scales = stage.tile([P, HALVES, P], U8, name="hid_scales", align_bytes=64)
+            nc.vector.quantize_mx(
+                out=codes[:].rearrange("q e b -> q (e b)").bitcast(FP8X4),
+                scales=scales[:].rearrange("q e b -> q (e b)"),
+                in_=hid_grouped[g][:].rearrange("q e b t -> q (e b t)"),
+            )
+            hid_codes[g] = (codes, scales)
+
+        def regroup_weights(g, e):
+            grouped = wstage.tile([P, HEAD_COLS, PACK], BF16, name="w_grouped", align_bytes=64)
+            nc.scalar.copy(
+                out=grouped[:, 0:CLS_COLS, :].rearrange("q (c i) t -> q c t i", i=4),
+                in_=cls_raw[g][:, :, e, :].rearrange("q t (c i) -> q c t i", i=4),
+            )
+            nc.vector.tensor_copy(
+                out=grouped[:, CLS_COLS:HEAD_COLS, :].rearrange("q (c i) t -> q c t i", i=4),
+                in_=box_raw[g][:, e].rearrange("q t (c i) -> q c t i", i=4),
+            )
+            w_grouped[(g, e)] = grouped
+
+        def head_pass(g, e):
+            flat_in = w_grouped[(g, e)][:].rearrange("q n t -> q (n t)")
+            codes = wstage.tile([P, HEAD_COLS], U32, name="w_codes", align_bytes=64)
+            scales = wstage.tile([P, HEAD_COLS], U8, name="w_scales", align_bytes=64)
+            h_codes, h_scales = hid_codes[g]
+            first = g == 0 and e == 0
+            last = g == CHUNKS - 1 and e == HALVES - 1
+            for lo, hi in ((0, WIDE), (WIDE, HEAD_COLS)):
+                nc.vector.quantize_mx(
+                    out=codes[:, lo:hi].bitcast(FP8X4),
+                    scales=scales[:, lo:hi],
+                    in_=flat_in[:, PACK * lo : PACK * hi],
+                )
+            for lo, hi, acc in ((0, WIDE, acc_wide), (WIDE, HEAD_COLS, acc_rest)):
+                nc.tensor.matmul_mx(
+                    out=acc[:],
+                    lhsT=h_codes[:, e, :].bitcast(FP8X4),
+                    lhsT_scale=h_scales[:, e, :],
+                    rhs=codes[:, lo:hi].bitcast(FP8X4),
+                    rhs_scale=scales[:, lo:hi],
+                    start=first,
+                    stop=last,
+                )
+
+        for step in range(CHUNKS + 2):
+            if step < CHUNKS:
+                transpose_features(step)
+            if 1 <= step <= CHUNKS:
+                quantise_features(step - 1)
+                convolve(step - 1)
+            if step >= 2:
+                quantise_hidden(step - 2)
+                for e in range(HALVES):
+                    regroup_weights(step - 2, e)
+                for e in range(HALVES):
+                    head_pass(step - 2, e)
+
+        lin = const.tile([P, 5, P], F32)
+        lin_flat = lin[:].rearrange("b c n -> b (c n)")
+        nc.vector.tensor_tensor(
+            out=lin_flat[:, 0:WIDE], in0=acc_wide[:], in1=bias_all[:, 0:WIDE], op=ALU.add
+        )
+        nc.vector.tensor_tensor(
+            out=lin_flat[:, WIDE:HEAD_COLS], in0=acc_rest[:], in1=bias_all[:, WIDE:HEAD_COLS], op=ALU.add
+        )
+        res = const.tile([P, 5, P], F32)
+        clipped = const.tile([P, 2, P], F32)
+        nc.vector.tensor_scalar(
+            out=clipped[:], in0=lin[:, 3:5, :], scalar1=-10.0, scalar2=10.0, op0=ALU.max, op1=ALU.min
+        )
+        grown = const.tile([P, 2, P], F32)
+        nc.scalar.activation(out=grown[:], in_=clipped[:], func=ACT.Exp)
+        margin = const.tile([P, P], F32)
+        nc.vector.tensor_tensor(out=margin[:], in0=lin[:, 1, :], in1=lin[:, 0, :], op=ALU.subtract)
+        squashed = const.tile([P, P], F32)
+        nc.scalar.activation(out=squashed[:], in_=margin[:], func=ACT.Tanh, scale=0.5)
+        shift = const.tile([P, P], F32)
+        nc.vector.tensor_tensor(out=shift[:], in0=lin[:, 2, :], in1=r[:, 3, :], op=ALU.mult)
+        nc.vector.tensor_tensor(out=res[:, 0, :], in0=r[:, 0, :], in1=shift[:], op=ALU.subtract)
+        nc.vector.tensor_copy(out=res[:, 1, :], in_=r[:, 1, :])
+        nc.vector.tensor_tensor(out=res[:, 2:4, :], in0=grown[:], in1=r[:, 2:4, :], op=ALU.mult)
+        nc.vector.tensor_scalar(
+            out=res[:, 4, :], in0=squashed[:], scalar1=0.5, scalar2=0.5, op0=ALU.mult, op1=ALU.add
+        )
+        packed = const.tile([P, P, 5], F32)
+        half = P // 2
+        nc.vector.tensor_copy(
+            out=packed[:, 0:half, :], in_=res[:, :, 0:half].rearrange("b c n -> b n c")
+        )
+        nc.scalar.copy(out=packed[:, half:P, :], in_=res[:, :, half:P].rearrange("b c n -> b n c"))
+        nc.sync.dma_start(out=out[:, 0:half, :], in_=packed[:, 0:half, :])
+        nc.sync.dma_start(out=out[:, half:P, :], in_=packed[:, half:P, :])

@@ -23,6 +23,7 @@ BOX_COLS = 384
 HEAD_COLS = CLS_COLS + BOX_COLS
 WIDE = 512
 STRIDE = 16.0
+STEPS = CHUNKS + 2
 
 FLOPS = 2 * P * POSITIONS * CHANNELS * HIDDEN + 2 * P * POSITIONS * HIDDEN * HEAD_COLS
 BYTES = (
@@ -40,56 +41,58 @@ def tile_classifiermodel_kernel(
         const = ctx.enter_context(tc.tile_pool(name="const", bufs=1))
         raw = ctx.enter_context(tc.tile_pool(name="raw", bufs=CHUNKS))
         stage = ctx.enter_context(tc.tile_pool(name="stage", bufs=3))
-        wstage = ctx.enter_context(tc.tile_pool(name="wstage", bufs=4))
+        wstage = ctx.enter_context(tc.tile_pool(name="wstage", bufs=6))
         psum_t = ctx.enter_context(tc.psum_pool(name="psum_t", bufs=4))
         psum_h = ctx.enter_context(tc.psum_pool(name="psum_h", bufs=2))
         psum_acc = ctx.enter_context(tc.psum_pool(name="psum_acc", bufs=1))
+        ctx.enter_context(tc.manual_schedule())
 
+        feat_rows = features.rearrange("b h w c -> b (h w) c")
+        feat_raw = {}
+        cls_raw = {}
+        box_raw = {}
+
+        def load_features(g):
+            feat_raw[g] = raw.tile([P, PACK, CHANNELS], BF16, name="feat_raw")
+            nc.sync.dma_start(out=feat_raw[g][:], in_=feat_rows[:, PACK * g : PACK * (g + 1), :])
+
+        def load_cls(g):
+            rows = slice(PACK * HIDDEN * g, PACK * HIDDEN * (g + 1))
+            cls_raw[g] = raw.tile([P, PACK, HALVES, CLS_COLS], BF16, name="cls_raw")
+            nc.sync.dma_start(
+                out=cls_raw[g][:],
+                in_=cls_w[rows, :].rearrange("(t q e) n -> q t e n", t=PACK, e=HALVES),
+            )
+
+        def load_box(g):
+            rows = slice(PACK * HIDDEN * g, PACK * HIDDEN * (g + 1))
+            box_raw[g] = raw.tile([P, HALVES, PACK, BOX_COLS], BF16, name="box_raw")
+            box_rows = bbox_w[rows, P:].rearrange("(t q e) n -> q e t n", t=PACK, e=HALVES)
+            for e in range(HALVES):
+                nc.sync.dma_start(out=box_raw[g][:, e], in_=box_rows[:, e])
+
+        load_features(0)
         cw_raw = const.tile([P, PACK, HIDDEN], BF16)
         nc.sync.dma_start(
             out=cw_raw[:].rearrange("q (u f) n -> q u f n", u=2),
             in_=conv_w.rearrange("(u q f) n -> q u f n", u=2, f=2),
         )
-
-        feat_rows = features.rearrange("b h w c -> b (h w) c")
-        feat_raw = []
-        cls_raw = []
-        box_raw = []
-
-        def load_features(g):
-            tile_f = raw.tile([P, PACK, CHANNELS], BF16, name="feat_raw")
-            nc.sync.dma_start(out=tile_f[:], in_=feat_rows[:, PACK * g : PACK * (g + 1), :])
-            feat_raw.append(tile_f)
-
-        def load_weights(g):
-            rows = slice(PACK * HIDDEN * g, PACK * HIDDEN * (g + 1))
-            tile_c = raw.tile([P, PACK, HALVES, CLS_COLS], BF16, name="cls_raw")
-            nc.sync.dma_start(
-                out=tile_c[:],
-                in_=cls_w[rows, :].rearrange("(t q e) n -> q t e n", t=PACK, e=HALVES),
-            )
-            cls_raw.append(tile_c)
-            tile_b = raw.tile([P, HALVES, PACK, BOX_COLS], BF16, name="box_raw")
-            box_rows = bbox_w[rows, P:].rearrange("(t q e) n -> q e t n", t=PACK, e=HALVES)
-            for e in range(HALVES):
-                nc.sync.dma_start(out=tile_b[:, e], in_=box_rows[:, e])
-            box_raw.append(tile_b)
-
-        load_features(0)
-        load_features(1)
-        for g in range(CHUNKS):
-            if g + 2 < CHUNKS:
-                load_features(g + 2)
-            load_weights(g)
+        for step in range(STEPS):
+            if step + 1 < CHUNKS:
+                load_features(step + 1)
+            if 0 <= step - 1 < CHUNKS:
+                load_cls(step - 1)
+            if 0 <= step - 2 < CHUNKS:
+                load_box(step - 2)
 
         convb_bf = const.tile([P, HALVES], BF16)
         nc.scalar.dma_start(out=convb_bf[:], in_=conv_b.rearrange("(q e) -> q e", e=HALVES))
-        roi_raw = const.tile([P, P, 4], BF16)
-        nc.scalar.dma_start(out=roi_raw[:], in_=roi)
         bias_rows = const.tile([P, HEAD_COLS], BF16)
         nc.vector.memset(bias_rows[:], 0.0)
         nc.scalar.dma_start(out=bias_rows[0:1, 0:CLS_COLS], in_=cls_b.unsqueeze(0))
         nc.scalar.dma_start(out=bias_rows[0:1, CLS_COLS:HEAD_COLS], in_=bbox_b[P:].unsqueeze(0))
+        roi_raw = const.tile([P, P, 4], BF16)
+        nc.scalar.dma_start(out=roi_raw[:], in_=roi)
 
         warm = const.tile([P, 1], F32)
         nc.vector.memset(warm[:], 0.0)
@@ -100,8 +103,130 @@ def tile_classifiermodel_kernel(
         ones = const.tile([P, P], BF16)
         nc.vector.memset(ones[:], 1.0)
 
-        convb = const.tile([P, HALVES], F32)
-        nc.vector.tensor_copy(out=convb[:], in_=convb_bf[:])
+        acc_wide = psum_acc.tile([P, WIDE], F32)
+        acc_rest = psum_acc.tile([P, HEAD_COLS - WIDE], F32)
+
+        feat_banks = {}
+        feat_grouped = {}
+        feat_codes = {}
+        hid_banks = {}
+        hid_grouped = {}
+        hid_codes = {}
+        w_grouped = {}
+        w_codes = {}
+
+        def transpose_features(g):
+            words = feat_raw[g][:].bitcast(F32)
+            for pair in range(2):
+                bank = psum_t.tile([P, 2, 2, P], F32, name="feat_t")
+                for t in range(2):
+                    for u in range(2):
+                        nc.tensor.transpose(
+                            bank[:, t, u, :], words[:, 2 * pair + t, P * u : P * (u + 1)], ident[:]
+                        )
+                feat_banks[(g, pair)] = bank
+
+        def group_features(g):
+            grouped = stage.tile([P, PACK * P, PACK], BF16, name="feat_grouped", align_bytes=64)
+            grouped_words = grouped[:].bitcast(F32)
+            for pair in range(2):
+                nc.scalar.copy(
+                    out=grouped_words[:, 2 * P * pair : 2 * P * (pair + 1), :].rearrange(
+                        "q (t b) u -> q t b u", t=2
+                    ),
+                    in_=feat_banks[(g, pair)][:].rearrange("q t u b -> q t b u"),
+                )
+            feat_grouped[g] = grouped
+
+        def quantise_features(g):
+            codes = stage.tile([P, PACK * P], U32, name="feat_codes", align_bytes=64)
+            scales = stage.tile([P, PACK * P], U8, name="feat_scales", align_bytes=64)
+            nc.vector.quantize_mx(
+                out=codes[:].bitcast(FP8X4),
+                scales=scales[:],
+                in_=feat_grouped[g][:].rearrange("q c k -> q (c k)"),
+            )
+            feat_codes[g] = (codes, scales)
+
+        def convolve(g):
+            codes, scales = feat_codes[g]
+            for e in range(HALVES):
+                hidden_ps = psum_h.tile([P, WIDE], F32, name="hidden_ps")
+                nc.tensor.matmul_mx(
+                    out=hidden_ps[:],
+                    lhsT=cw_codes[:, P * e : P * (e + 1)].bitcast(FP8X4),
+                    lhsT_scale=cw_scales[:, P * e : P * (e + 1)],
+                    rhs=codes[:].bitcast(FP8X4),
+                    rhs_scale=scales[:],
+                    start=True,
+                    stop=True,
+                )
+                hid_banks[(g, e)] = hidden_ps
+
+        def group_hidden(g):
+            grouped = stage.tile([P, HALVES, P, PACK], BF16, name="hid_grouped", align_bytes=64)
+            for e in range(HALVES):
+                nc.scalar.activation(
+                    out=grouped[:, e],
+                    in_=hid_banks[(g, e)][:].rearrange("q (t b) -> q b t", t=PACK),
+                    func=ACT.Relu,
+                    bias=convb[:, e : e + 1],
+                )
+            hid_grouped[g] = grouped
+
+        def quantise_hidden(g):
+            codes = stage.tile([P, HALVES, P], U32, name="hid_codes", align_bytes=64)
+            scales = stage.tile([P, HALVES, P], U8, name="hid_scales", align_bytes=64)
+            nc.vector.quantize_mx(
+                out=codes[:].rearrange("q e b -> q (e b)").bitcast(FP8X4),
+                scales=scales[:].rearrange("q e b -> q (e b)"),
+                in_=hid_grouped[g][:].rearrange("q e b t -> q (e b t)"),
+            )
+            hid_codes[g] = (codes, scales)
+
+        def group_cls(g, e):
+            grouped = wstage.tile([P, HEAD_COLS, PACK], BF16, name="w_grouped", align_bytes=64)
+            nc.scalar.copy(
+                out=grouped[:, 0:CLS_COLS, :].rearrange("q (c i) t -> q c t i", i=4),
+                in_=cls_raw[g][:, :, e, :].rearrange("q t (c i) -> q c t i", i=4),
+            )
+            w_grouped[(g, e)] = grouped
+
+        def group_box(g, e):
+            nc.vector.tensor_copy(
+                out=w_grouped[(g, e)][:, CLS_COLS:HEAD_COLS, :].rearrange(
+                    "q (c i) t -> q c t i", i=4
+                ),
+                in_=box_raw[g][:, e].rearrange("q t (c i) -> q c t i", i=4),
+            )
+
+        def quantise_weights(g, e):
+            flat_in = w_grouped[(g, e)][:].rearrange("q n t -> q (n t)")
+            codes = wstage.tile([P, HEAD_COLS], U32, name="w_codes", align_bytes=64)
+            scales = wstage.tile([P, HEAD_COLS], U8, name="w_scales", align_bytes=64)
+            for lo, hi in ((0, WIDE), (WIDE, HEAD_COLS)):
+                nc.vector.quantize_mx(
+                    out=codes[:, lo:hi].bitcast(FP8X4),
+                    scales=scales[:, lo:hi],
+                    in_=flat_in[:, PACK * lo : PACK * hi],
+                )
+            w_codes[(g, e)] = (codes, scales)
+
+        def head_pass(g, e):
+            codes, scales = w_codes[(g, e)]
+            h_codes, h_scales = hid_codes[g]
+            for lo, hi, acc in ((0, WIDE, acc_wide), (WIDE, HEAD_COLS, acc_rest)):
+                nc.tensor.matmul_mx(
+                    out=acc[:],
+                    lhsT=h_codes[:, e, :].bitcast(FP8X4),
+                    lhsT_scale=h_scales[:, e, :],
+                    rhs=codes[:, lo:hi].bitcast(FP8X4),
+                    rhs_scale=scales[:, lo:hi],
+                    start=(g == 0 and e == 0),
+                    stop=(g == CHUNKS - 1 and e == HALVES - 1),
+                )
+
+        transpose_features(0)
 
         cw_grouped = const.tile([P, HIDDEN, PACK], BF16, align_bytes=64)
         for e in range(HALVES):
@@ -109,6 +234,8 @@ def tile_classifiermodel_kernel(
                 out=cw_grouped[:, P * e : P * (e + 1), :],
                 in_=cw_raw[:].rearrange("q k (m e) -> q e m k", e=HALVES)[:, e],
             )
+        convb = const.tile([P, HALVES], F32)
+        nc.vector.tensor_copy(out=convb[:], in_=convb_bf[:])
         cw_codes = const.tile([P, HIDDEN], U32, align_bytes=64)
         cw_scales = const.tile([P, HIDDEN], U8, align_bytes=64)
         nc.vector.quantize_mx(
@@ -133,141 +260,49 @@ def tile_classifiermodel_kernel(
             scalar2=None,
             op0=ALU.mult,
         )
+        res = const.tile([P, 5, P], F32)
+        nc.vector.tensor_copy(out=res[:, 1, :], in_=r[:, 1, :])
 
-        acc_wide = psum_acc.tile([P, WIDE], F32)
-        acc_rest = psum_acc.tile([P, HEAD_COLS - WIDE], F32)
-
-        feat_grouped = {}
-        feat_codes = {}
-        hid_grouped = {}
-        hid_codes = {}
-        w_grouped = {}
-
-        def transpose_features(g):
-            words = feat_raw[g][:].bitcast(F32)
-            grouped = stage.tile([P, PACK * P, PACK], BF16, name="feat_grouped", align_bytes=64)
-            grouped_words = grouped[:].bitcast(F32)
-            for pair in range(2):
-                bank = psum_t.tile([P, 2, 2, P], F32, name="feat_t")
-                for t in range(2):
-                    for u in range(2):
-                        nc.tensor.transpose(
-                            bank[:, t, u, :], words[:, 2 * pair + t, P * u : P * (u + 1)], ident[:]
-                        )
-                nc.scalar.copy(
-                    out=grouped_words[:, 2 * P * pair : 2 * P * (pair + 1), :].rearrange(
-                        "q (t b) u -> q t b u", t=2
-                    ),
-                    in_=bank[:].rearrange("q t u b -> q t b u"),
-                )
-            feat_grouped[g] = grouped
-
-        def quantise_features(g):
-            codes = stage.tile([P, PACK * P], U32, name="feat_codes", align_bytes=64)
-            scales = stage.tile([P, PACK * P], U8, name="feat_scales", align_bytes=64)
-            nc.vector.quantize_mx(
-                out=codes[:].bitcast(FP8X4),
-                scales=scales[:],
-                in_=feat_grouped[g][:].rearrange("q c k -> q (c k)"),
-            )
-            feat_codes[g] = (codes, scales)
-
-        def convolve(g):
-            codes, scales = feat_codes[g]
-            grouped = stage.tile([P, HALVES, P, PACK], BF16, name="hid_grouped", align_bytes=64)
-            for e in range(HALVES):
-                hidden_ps = psum_h.tile([P, WIDE], F32, name="hidden_ps")
-                nc.tensor.matmul_mx(
-                    out=hidden_ps[:],
-                    lhsT=cw_codes[:, P * e : P * (e + 1)].bitcast(FP8X4),
-                    lhsT_scale=cw_scales[:, P * e : P * (e + 1)],
-                    rhs=codes[:].bitcast(FP8X4),
-                    rhs_scale=scales[:],
-                    start=True,
-                    stop=True,
-                )
-                nc.scalar.activation(
-                    out=grouped[:, e],
-                    in_=hidden_ps[:].rearrange("q (t b) -> q b t", t=PACK),
-                    func=ACT.Relu,
-                    bias=convb[:, e : e + 1],
-                )
-            hid_grouped[g] = grouped
-
-        def quantise_hidden(g):
-            codes = stage.tile([P, HALVES, P], U32, name="hid_codes", align_bytes=64)
-            scales = stage.tile([P, HALVES, P], U8, name="hid_scales", align_bytes=64)
-            nc.vector.quantize_mx(
-                out=codes[:].rearrange("q e b -> q (e b)").bitcast(FP8X4),
-                scales=scales[:].rearrange("q e b -> q (e b)"),
-                in_=hid_grouped[g][:].rearrange("q e b t -> q (e b t)"),
-            )
-            hid_codes[g] = (codes, scales)
-
-        def regroup_weights(g, e):
-            grouped = wstage.tile([P, HEAD_COLS, PACK], BF16, name="w_grouped", align_bytes=64)
-            nc.scalar.copy(
-                out=grouped[:, 0:CLS_COLS, :].rearrange("q (c i) t -> q c t i", i=4),
-                in_=cls_raw[g][:, :, e, :].rearrange("q t (c i) -> q c t i", i=4),
-            )
-            nc.vector.tensor_copy(
-                out=grouped[:, CLS_COLS:HEAD_COLS, :].rearrange("q (c i) t -> q c t i", i=4),
-                in_=box_raw[g][:, e].rearrange("q t (c i) -> q c t i", i=4),
-            )
-            w_grouped[(g, e)] = grouped
-
-        def head_pass(g, e):
-            flat_in = w_grouped[(g, e)][:].rearrange("q n t -> q (n t)")
-            codes = wstage.tile([P, HEAD_COLS], U32, name="w_codes", align_bytes=64)
-            scales = wstage.tile([P, HEAD_COLS], U8, name="w_scales", align_bytes=64)
-            h_codes, h_scales = hid_codes[g]
-            first = g == 0 and e == 0
-            last = g == CHUNKS - 1 and e == HALVES - 1
-            for lo, hi in ((0, WIDE), (WIDE, HEAD_COLS)):
-                nc.vector.quantize_mx(
-                    out=codes[:, lo:hi].bitcast(FP8X4),
-                    scales=scales[:, lo:hi],
-                    in_=flat_in[:, PACK * lo : PACK * hi],
-                )
-            for lo, hi, acc in ((0, WIDE, acc_wide), (WIDE, HEAD_COLS, acc_rest)):
-                nc.tensor.matmul_mx(
-                    out=acc[:],
-                    lhsT=h_codes[:, e, :].bitcast(FP8X4),
-                    lhsT_scale=h_scales[:, e, :],
-                    rhs=codes[:, lo:hi].bitcast(FP8X4),
-                    rhs_scale=scales[:, lo:hi],
-                    start=first,
-                    stop=last,
-                )
-
-        for step in range(CHUNKS + 2):
+        for step in range(STEPS):
+            conv_chunk = step - 1
+            head_chunk = step - 2
+            if 0 <= conv_chunk < CHUNKS:
+                quantise_features(conv_chunk)
+                convolve(conv_chunk)
+            if step + 1 < CHUNKS:
+                transpose_features(step + 1)
             if step < CHUNKS:
-                transpose_features(step)
-            if 1 <= step <= CHUNKS:
-                quantise_features(step - 1)
-                convolve(step - 1)
-            if step >= 2:
-                quantise_hidden(step - 2)
+                group_features(step)
+            if 0 <= conv_chunk < CHUNKS:
+                group_cls(conv_chunk, 0)
+                group_hidden(conv_chunk)
+                group_cls(conv_chunk, 1)
+            if 0 <= head_chunk < CHUNKS:
+                group_box(head_chunk, 0)
+                quantise_hidden(head_chunk)
+                group_box(head_chunk, 1)
                 for e in range(HALVES):
-                    regroup_weights(step - 2, e)
-                for e in range(HALVES):
-                    head_pass(step - 2, e)
+                    quantise_weights(head_chunk, e)
+                    head_pass(head_chunk, e)
 
         lin = const.tile([P, 5, P], F32)
         lin_flat = lin[:].rearrange("b c n -> b (c n)")
+        exp_lo = 3 * P
         nc.vector.tensor_tensor(
-            out=lin_flat[:, 0:WIDE], in0=acc_wide[:], in1=bias_all[:, 0:WIDE], op=ALU.add
+            out=lin_flat[:, exp_lo:WIDE], in0=acc_wide[:, exp_lo:WIDE], in1=bias_all[:, exp_lo:WIDE], op=ALU.add
         )
         nc.vector.tensor_tensor(
             out=lin_flat[:, WIDE:HEAD_COLS], in0=acc_rest[:], in1=bias_all[:, WIDE:HEAD_COLS], op=ALU.add
         )
-        res = const.tile([P, 5, P], F32)
         clipped = const.tile([P, 2, P], F32)
         nc.vector.tensor_scalar(
             out=clipped[:], in0=lin[:, 3:5, :], scalar1=-10.0, scalar2=10.0, op0=ALU.max, op1=ALU.min
         )
         grown = const.tile([P, 2, P], F32)
         nc.scalar.activation(out=grown[:], in_=clipped[:], func=ACT.Exp)
+        nc.vector.tensor_tensor(
+            out=lin_flat[:, 0:exp_lo], in0=acc_wide[:, 0:exp_lo], in1=bias_all[:, 0:exp_lo], op=ALU.add
+        )
         margin = const.tile([P, P], F32)
         nc.vector.tensor_tensor(out=margin[:], in0=lin[:, 1, :], in1=lin[:, 0, :], op=ALU.subtract)
         squashed = const.tile([P, P], F32)
@@ -275,7 +310,6 @@ def tile_classifiermodel_kernel(
         shift = const.tile([P, P], F32)
         nc.vector.tensor_tensor(out=shift[:], in0=lin[:, 2, :], in1=r[:, 3, :], op=ALU.mult)
         nc.vector.tensor_tensor(out=res[:, 0, :], in0=r[:, 0, :], in1=shift[:], op=ALU.subtract)
-        nc.vector.tensor_copy(out=res[:, 1, :], in_=r[:, 1, :])
         nc.vector.tensor_tensor(out=res[:, 2:4, :], in0=grown[:], in1=r[:, 2:4, :], op=ALU.mult)
         nc.vector.tensor_scalar(
             out=res[:, 4, :], in0=squashed[:], scalar1=0.5, scalar2=0.5, op0=ALU.mult, op1=ALU.add

@@ -23,7 +23,6 @@ BOX_COLS = 384
 HEAD_COLS = CLS_COLS + BOX_COLS
 WIDE = 512
 STRIDE = 16.0
-STEPS = CHUNKS + 2
 
 FLOPS = 2 * P * POSITIONS * CHANNELS * HIDDEN + 2 * P * POSITIONS * HIDDEN * HEAD_COLS
 BYTES = (
@@ -41,7 +40,7 @@ def tile_classifiermodel_kernel(
         const = ctx.enter_context(tc.tile_pool(name="const", bufs=1))
         raw = ctx.enter_context(tc.tile_pool(name="raw", bufs=CHUNKS))
         stage = ctx.enter_context(tc.tile_pool(name="stage", bufs=3))
-        wstage = ctx.enter_context(tc.tile_pool(name="wstage", bufs=6))
+        wstage = ctx.enter_context(tc.tile_pool(name="wstage", bufs=4))
         psum_t = ctx.enter_context(tc.psum_pool(name="psum_t", bufs=4))
         psum_h = ctx.enter_context(tc.psum_pool(name="psum_h", bufs=2))
         psum_acc = ctx.enter_context(tc.psum_pool(name="psum_acc", bufs=1))
@@ -64,12 +63,11 @@ def tile_classifiermodel_kernel(
                 in_=cls_w[rows, :].rearrange("(t q e) n -> q t e n", t=PACK, e=HALVES),
             )
 
-        def load_box(g):
+        def load_box(g, e):
             rows = slice(PACK * HIDDEN * g, PACK * HIDDEN * (g + 1))
-            box_raw[g] = raw.tile([P, HALVES, PACK, BOX_COLS], BF16, name="box_raw")
+            box_raw[(g, e)] = raw.tile([P, PACK, BOX_COLS], BF16, name="box_raw", bufs=HALVES * CHUNKS)
             box_rows = bbox_w[rows, P:].rearrange("(t q e) n -> q e t n", t=PACK, e=HALVES)
-            for e in range(HALVES):
-                nc.sync.dma_start(out=box_raw[g][:, e], in_=box_rows[:, e])
+            nc.sync.dma_start(out=box_raw[(g, e)][:], in_=box_rows[:, e])
 
         load_features(0)
         cw_raw = const.tile([P, PACK, HIDDEN], BF16)
@@ -77,13 +75,12 @@ def tile_classifiermodel_kernel(
             out=cw_raw[:].rearrange("q (u f) n -> q u f n", u=2),
             in_=conv_w.rearrange("(u q f) n -> q u f n", u=2, f=2),
         )
-        for step in range(STEPS):
-            if step + 1 < CHUNKS:
-                load_features(step + 1)
-            if 0 <= step - 1 < CHUNKS:
-                load_cls(step - 1)
-            if 0 <= step - 2 < CHUNKS:
-                load_box(step - 2)
+        for g in range(CHUNKS):
+            load_cls(g)
+            load_box(g, 0)
+            if g + 1 < CHUNKS:
+                load_features(g + 1)
+            load_box(g, 1)
 
         convb_bf = const.tile([P, HALVES], BF16)
         nc.scalar.dma_start(out=convb_bf[:], in_=conv_b.rearrange("(q e) -> q e", e=HALVES))
@@ -185,19 +182,17 @@ def tile_classifiermodel_kernel(
             hid_codes[g] = (codes, scales)
 
         def group_cls(g, e):
-            grouped = wstage.tile([P, HEAD_COLS, PACK], BF16, name="w_grouped", align_bytes=64)
             nc.scalar.copy(
-                out=grouped[:, 0:CLS_COLS, :].rearrange("q (c i) t -> q c t i", i=4),
+                out=w_grouped[(g, e)][:, 0:CLS_COLS, :].rearrange("q (c i) t -> q c t i", i=4),
                 in_=cls_raw[g][:, :, e, :].rearrange("q t (c i) -> q c t i", i=4),
             )
-            w_grouped[(g, e)] = grouped
 
         def group_box(g, e):
             nc.vector.tensor_copy(
                 out=w_grouped[(g, e)][:, CLS_COLS:HEAD_COLS, :].rearrange(
                     "q (c i) t -> q c t i", i=4
                 ),
-                in_=box_raw[g][:, e].rearrange("q t (c i) -> q c t i", i=4),
+                in_=box_raw[(g, e)][:].rearrange("q t (c i) -> q c t i", i=4),
             )
 
         def quantise_weights(g, e):
@@ -263,27 +258,30 @@ def tile_classifiermodel_kernel(
         res = const.tile([P, 5, P], F32)
         nc.vector.tensor_copy(out=res[:, 1, :], in_=r[:, 1, :])
 
-        for step in range(STEPS):
-            conv_chunk = step - 1
-            head_chunk = step - 2
-            if 0 <= conv_chunk < CHUNKS:
-                quantise_features(conv_chunk)
-                convolve(conv_chunk)
-            if step + 1 < CHUNKS:
-                transpose_features(step + 1)
-            if step < CHUNKS:
-                group_features(step)
-            if 0 <= conv_chunk < CHUNKS:
-                group_cls(conv_chunk, 0)
-                group_hidden(conv_chunk)
-                group_cls(conv_chunk, 1)
-            if 0 <= head_chunk < CHUNKS:
-                group_box(head_chunk, 0)
-                quantise_hidden(head_chunk)
-                group_box(head_chunk, 1)
-                for e in range(HALVES):
-                    quantise_weights(head_chunk, e)
-                    head_pass(head_chunk, e)
+        group_features(0)
+        for g in range(CHUNKS):
+            for e in range(HALVES):
+                w_grouped[(g, e)] = wstage.tile(
+                    [P, HEAD_COLS, PACK], BF16, name="w_grouped", align_bytes=64
+                )
+            quantise_features(g)
+            convolve(g)
+            group_cls(g, 0)
+            group_box(g, 0)
+            group_hidden(g)
+            if g + 1 < CHUNKS:
+                transpose_features(g + 1)
+                group_features(g + 1)
+            if g > 0:
+                quantise_weights(g - 1, 1)
+                head_pass(g - 1, 1)
+            group_box(g, 1)
+            group_cls(g, 1)
+            quantise_hidden(g)
+            quantise_weights(g, 0)
+            head_pass(g, 0)
+        quantise_weights(CHUNKS - 1, 1)
+        head_pass(CHUNKS - 1, 1)
 
         lin = const.tile([P, 5, P], F32)
         lin_flat = lin[:].rearrange("b c n -> b (c n)")

@@ -22,6 +22,8 @@ CLS_COLS = 256
 BOX_COLS = 384
 HEAD_COLS = CLS_COLS + BOX_COLS
 WIDE = 512
+B1 = CLS_COLS
+B2 = CLS_COLS + P
 STRIDE = 16.0
 
 FLOPS = 2 * P * POSITIONS * CHANNELS * HIDDEN + 2 * P * POSITIONS * HIDDEN * HEAD_COLS
@@ -41,7 +43,7 @@ def tile_classifiermodel_kernel(
         raw = ctx.enter_context(tc.tile_pool(name="raw", bufs=CHUNKS))
         stage = ctx.enter_context(tc.tile_pool(name="stage", bufs=3))
         wstage = ctx.enter_context(tc.tile_pool(name="wstage", bufs=4))
-        psum_t = ctx.enter_context(tc.psum_pool(name="psum_t", bufs=4))
+        psum_t = ctx.enter_context(tc.psum_pool(name="psum_t", bufs=3))
         psum_h = ctx.enter_context(tc.psum_pool(name="psum_h", bufs=2))
         psum_acc = ctx.enter_context(tc.psum_pool(name="psum_acc", bufs=1))
         ctx.enter_context(tc.manual_schedule())
@@ -53,7 +55,12 @@ def tile_classifiermodel_kernel(
 
         def load_features(g):
             feat_raw[g] = raw.tile([P, PACK, CHANNELS], BF16, name="feat_raw")
-            nc.sync.dma_start(out=feat_raw[g][:], in_=feat_rows[:, PACK * g : PACK * (g + 1), :])
+            load_positions(g, 0, PACK)
+
+        def load_positions(g, lo, hi):
+            nc.sync.dma_start(
+                out=feat_raw[g][:, lo:hi, :], in_=feat_rows[:, PACK * g + lo : PACK * g + hi, :]
+            )
 
         def load_cls(g):
             rows = slice(PACK * HIDDEN * g, PACK * HIDDEN * (g + 1))
@@ -69,27 +76,30 @@ def tile_classifiermodel_kernel(
             box_rows = bbox_w[rows, P:].rearrange("(t q e) n -> q e t n", t=PACK, e=HALVES)
             nc.sync.dma_start(out=box_raw[(g, e)][:], in_=box_rows[:, e])
 
-        load_features(0)
+        feat_raw[0] = raw.tile([P, PACK, CHANNELS], BF16, name="feat_raw")
+        load_positions(0, 0, 2)
         cw_raw = const.tile([P, PACK, HIDDEN], BF16)
         nc.sync.dma_start(
             out=cw_raw[:].rearrange("q (u f) n -> q u f n", u=2),
             in_=conv_w.rearrange("(u q f) n -> q u f n", u=2, f=2),
         )
+        load_positions(0, 2, PACK)
+        roi_raw = const.tile([P, P, 4], BF16)
         for g in range(CHUNKS):
             load_cls(g)
             load_box(g, 0)
             if g + 1 < CHUNKS:
                 load_features(g + 1)
             load_box(g, 1)
+            if g == 1:
+                nc.sync.dma_start(out=roi_raw[:], in_=roi)
 
-        convb_bf = const.tile([P, HALVES], BF16)
-        nc.scalar.dma_start(out=convb_bf[:], in_=conv_b.rearrange("(q e) -> q e", e=HALVES))
         bias_rows = const.tile([P, HEAD_COLS], BF16)
         nc.vector.memset(bias_rows[:], 0.0)
         nc.scalar.dma_start(out=bias_rows[0:1, 0:CLS_COLS], in_=cls_b.unsqueeze(0))
         nc.scalar.dma_start(out=bias_rows[0:1, CLS_COLS:HEAD_COLS], in_=bbox_b[P:].unsqueeze(0))
-        roi_raw = const.tile([P, P, 4], BF16)
-        nc.scalar.dma_start(out=roi_raw[:], in_=roi)
+        convb_bf = const.tile([P, HALVES], BF16)
+        nc.scalar.dma_start(out=convb_bf[:], in_=conv_b.rearrange("(q e) -> q e", e=HALVES))
 
         warm = const.tile([P, 1], F32)
         nc.vector.memset(warm[:], 0.0)
@@ -100,8 +110,9 @@ def tile_classifiermodel_kernel(
         ones = const.tile([P, P], BF16)
         nc.vector.memset(ones[:], 1.0)
 
-        acc_wide = psum_acc.tile([P, WIDE], F32)
-        acc_rest = psum_acc.tile([P, HEAD_COLS - WIDE], F32)
+        acc_cls = psum_acc.tile([P, CLS_COLS], F32)
+        acc_shift = psum_acc.tile([P, P], F32)
+        acc_size = psum_acc.tile([P, 2 * P], F32)
 
         feat_banks = {}
         feat_grouped = {}
@@ -195,22 +206,28 @@ def tile_classifiermodel_kernel(
                 in_=box_raw[(g, e)][:].rearrange("q t (c i) -> q c t i", i=4),
             )
 
-        def quantise_weights(g, e):
-            flat_in = w_grouped[(g, e)][:].rearrange("q n t -> q (n t)")
+        def weight_tiles(g, e):
+            w_grouped[(g, e)] = wstage.tile(
+                [P, HEAD_COLS, PACK], BF16, name="w_grouped", align_bytes=64
+            )
             codes = wstage.tile([P, HEAD_COLS], U32, name="w_codes", align_bytes=64)
             scales = wstage.tile([P, HEAD_COLS], U8, name="w_scales", align_bytes=64)
-            for lo, hi in ((0, WIDE), (WIDE, HEAD_COLS)):
+            w_codes[(g, e)] = (codes, scales)
+
+        def quantise_weights(g, e, columns):
+            flat_in = w_grouped[(g, e)][:].rearrange("q n t -> q (n t)")
+            codes, scales = w_codes[(g, e)]
+            for lo, hi in columns:
                 nc.vector.quantize_mx(
                     out=codes[:, lo:hi].bitcast(FP8X4),
                     scales=scales[:, lo:hi],
                     in_=flat_in[:, PACK * lo : PACK * hi],
                 )
-            w_codes[(g, e)] = (codes, scales)
 
-        def head_pass(g, e):
+        def head_pass(g, e, sums):
             codes, scales = w_codes[(g, e)]
             h_codes, h_scales = hid_codes[g]
-            for lo, hi, acc in ((0, WIDE, acc_wide), (WIDE, HEAD_COLS, acc_rest)):
+            for lo, hi, acc in sums:
                 nc.tensor.matmul_mx(
                     out=acc[:],
                     lhsT=h_codes[:, e, :].bitcast(FP8X4),
@@ -220,6 +237,14 @@ def tile_classifiermodel_kernel(
                     start=(g == 0 and e == 0),
                     stop=(g == CHUNKS - 1 and e == HALVES - 1),
                 )
+
+        bias_all = const.tile([P, HEAD_COLS], F32)
+        for lo, hi in ((0, WIDE), (WIDE, HEAD_COLS)):
+            spread = psum_h.tile([P, WIDE], F32, name="hidden_ps")
+            nc.tensor.matmul(
+                out=spread[:, 0 : hi - lo], lhsT=ones[:], rhs=bias_rows[:, lo:hi], start=True, stop=True
+            )
+            nc.scalar.copy(out=bias_all[:, lo:hi], in_=spread[:, 0 : hi - lo])
 
         transpose_features(0)
 
@@ -239,31 +264,20 @@ def tile_classifiermodel_kernel(
             in_=cw_grouped[:].rearrange("q n k -> q (n k)"),
         )
 
-        bias_all = const.tile([P, HEAD_COLS], F32)
-        for lo, hi in ((0, WIDE), (WIDE, HEAD_COLS)):
-            spread = psum_h.tile([P, WIDE], F32, name="hidden_ps")
-            nc.tensor.matmul(
-                out=spread[:, 0 : hi - lo], lhsT=ones[:], rhs=bias_rows[:, lo:hi], start=True, stop=True
-            )
-            nc.vector.tensor_copy(out=bias_all[:, lo:hi], in_=spread[:, 0 : hi - lo])
-
+        all_columns = ((0, WIDE), (WIDE, HEAD_COLS))
+        cls_sums = (0, B1, acc_cls)
+        shift_sums = (B1, B2, acc_shift)
+        size_sums = (B2, HEAD_COLS, acc_size)
+        all_sums = (cls_sums, shift_sums, size_sums)
+        last = CHUNKS - 1
         r = const.tile([P, 4, P], F32)
-        nc.vector.tensor_scalar(
-            out=r[:],
-            in0=roi_raw[:].rearrange("b n c -> b c n"),
-            scalar1=STRIDE,
-            scalar2=None,
-            op0=ALU.mult,
-        )
         res = const.tile([P, 5, P], F32)
-        nc.vector.tensor_copy(out=res[:, 1, :], in_=r[:, 1, :])
+        lin = const.tile([P, HEAD_COLS], F32)
 
         group_features(0)
         for g in range(CHUNKS):
-            for e in range(HALVES):
-                w_grouped[(g, e)] = wstage.tile(
-                    [P, HEAD_COLS, PACK], BF16, name="w_grouped", align_bytes=64
-                )
+            weight_tiles(g, 0)
+            weight_tiles(g, 1)
             quantise_features(g)
             convolve(g)
             group_cls(g, 0)
@@ -273,45 +287,68 @@ def tile_classifiermodel_kernel(
                 transpose_features(g + 1)
                 group_features(g + 1)
             if g > 0:
-                quantise_weights(g - 1, 1)
-                head_pass(g - 1, 1)
-            group_box(g, 1)
+                quantise_weights(g - 1, 1, all_columns)
+                head_pass(g - 1, 1, all_sums)
+            if g < last:
+                group_box(g, 1)
             group_cls(g, 1)
             quantise_hidden(g)
-            quantise_weights(g, 0)
-            head_pass(g, 0)
-        quantise_weights(CHUNKS - 1, 1)
-        head_pass(CHUNKS - 1, 1)
+            quantise_weights(g, 0, all_columns)
+            head_pass(g, 0, all_sums)
+            if g == 2:
+                nc.vector.tensor_scalar(
+                    out=r[:],
+                    in0=roi_raw[:].rearrange("b n c -> b c n"),
+                    scalar1=STRIDE,
+                    scalar2=None,
+                    op0=ALU.mult,
+                )
+                nc.vector.tensor_copy(out=res[:, 1, :], in_=r[:, 1, :])
 
-        lin = const.tile([P, 5, P], F32)
-        lin_flat = lin[:].rearrange("b c n -> b (c n)")
-        exp_lo = 3 * P
+        grouped = w_grouped[(last, 1)]
+
+        def last_box(copy, lo, hi):
+            copy(
+                out=grouped[:, CLS_COLS + lo : CLS_COLS + hi, :].rearrange("q (c i) t -> q c t i", i=4),
+                in_=box_raw[(last, 1)][:, :, lo:hi].rearrange("q t (c i) -> q c t i", i=4),
+            )
+
+        last_box(nc.vector.tensor_copy, P, BOX_COLS)
+        last_box(nc.scalar.copy, 0, P)
+        quantise_weights(last, 1, ((0, B1),))
+        head_pass(last, 1, (cls_sums,))
+        quantise_weights(last, 1, ((B2, HEAD_COLS),))
+        head_pass(last, 1, (size_sums,))
+        quantise_weights(last, 1, ((B1, B2),))
+        head_pass(last, 1, (shift_sums,))
+
+        nc.vector.tensor_tensor(out=lin[:, 0:B1], in0=acc_cls[:], in1=bias_all[:, 0:B1], op=ALU.add)
         nc.vector.tensor_tensor(
-            out=lin_flat[:, exp_lo:WIDE], in0=acc_wide[:, exp_lo:WIDE], in1=bias_all[:, exp_lo:WIDE], op=ALU.add
-        )
-        nc.vector.tensor_tensor(
-            out=lin_flat[:, WIDE:HEAD_COLS], in0=acc_rest[:], in1=bias_all[:, WIDE:HEAD_COLS], op=ALU.add
-        )
-        clipped = const.tile([P, 2, P], F32)
-        nc.vector.tensor_scalar(
-            out=clipped[:], in0=lin[:, 3:5, :], scalar1=-10.0, scalar2=10.0, op0=ALU.max, op1=ALU.min
-        )
-        grown = const.tile([P, 2, P], F32)
-        nc.scalar.activation(out=grown[:], in_=clipped[:], func=ACT.Exp)
-        nc.vector.tensor_tensor(
-            out=lin_flat[:, 0:exp_lo], in0=acc_wide[:, 0:exp_lo], in1=bias_all[:, 0:exp_lo], op=ALU.add
+            out=lin[:, B2:HEAD_COLS], in0=acc_size[:], in1=bias_all[:, B2:HEAD_COLS], op=ALU.add
         )
         margin = const.tile([P, P], F32)
-        nc.vector.tensor_tensor(out=margin[:], in0=lin[:, 1, :], in1=lin[:, 0, :], op=ALU.subtract)
+        nc.vector.tensor_tensor(out=margin[:], in0=lin[:, P : 2 * P], in1=lin[:, 0:P], op=ALU.subtract)
+        clipped = const.tile([P, 2, P], F32)
+        nc.vector.tensor_scalar(
+            out=clipped[:].rearrange("b c n -> b (c n)"),
+            in0=lin[:, B2:HEAD_COLS],
+            scalar1=-10.0,
+            scalar2=10.0,
+            op0=ALU.max,
+            op1=ALU.min,
+        )
         squashed = const.tile([P, P], F32)
         nc.scalar.activation(out=squashed[:], in_=margin[:], func=ACT.Tanh, scale=0.5)
-        shift = const.tile([P, P], F32)
-        nc.vector.tensor_tensor(out=shift[:], in0=lin[:, 2, :], in1=r[:, 3, :], op=ALU.mult)
-        nc.vector.tensor_tensor(out=res[:, 0, :], in0=r[:, 0, :], in1=shift[:], op=ALU.subtract)
-        nc.vector.tensor_tensor(out=res[:, 2:4, :], in0=grown[:], in1=r[:, 2:4, :], op=ALU.mult)
+        grown = const.tile([P, 2, P], F32)
+        nc.scalar.activation(out=grown[:], in_=clipped[:], func=ACT.Exp)
+        nc.vector.tensor_tensor(out=lin[:, B1:B2], in0=acc_shift[:], in1=bias_all[:, B1:B2], op=ALU.add)
         nc.vector.tensor_scalar(
             out=res[:, 4, :], in0=squashed[:], scalar1=0.5, scalar2=0.5, op0=ALU.mult, op1=ALU.add
         )
+        shift = const.tile([P, P], F32)
+        nc.vector.tensor_tensor(out=shift[:], in0=lin[:, B1:B2], in1=r[:, 3, :], op=ALU.mult)
+        nc.vector.tensor_tensor(out=res[:, 2:4, :], in0=grown[:], in1=r[:, 2:4, :], op=ALU.mult)
+        nc.vector.tensor_tensor(out=res[:, 0, :], in0=r[:, 0, :], in1=shift[:], op=ALU.subtract)
         packed = const.tile([P, P, 5], F32)
         half = P // 2
         nc.vector.tensor_copy(

@@ -76,6 +76,11 @@ def tile_classifiermodel_kernel(
             box_rows = bbox_w[rows, P:].rearrange("(t q e) n -> q e t n", t=PACK, e=HALVES)
             nc.sync.dma_start(out=box_raw[(g, e)][:], in_=box_rows[:, e])
 
+        bias_rows = const.tile([P, HEAD_COLS], BF16)
+        nc.vector.memset(bias_rows[:], 0.0)
+        nc.sync.dma_start(out=bias_rows[0:1, 0:CLS_COLS], in_=cls_b.unsqueeze(0))
+        nc.sync.dma_start(out=bias_rows[0:1, CLS_COLS:HEAD_COLS], in_=bbox_b[P:].unsqueeze(0))
+
         feat_raw[0] = raw.tile([P, PACK, CHANNELS], BF16, name="feat_raw")
         load_positions(0, 0, 2)
         cw_raw = const.tile([P, PACK, HIDDEN], BF16)
@@ -87,17 +92,15 @@ def tile_classifiermodel_kernel(
         roi_raw = const.tile([P, P, 4], BF16)
         for g in range(CHUNKS):
             load_cls(g)
+            if g == 0:
+                load_features(1)
             load_box(g, 0)
-            if g + 1 < CHUNKS:
-                load_features(g + 1)
             load_box(g, 1)
+            if g + 2 < CHUNKS:
+                load_features(g + 2)
             if g == 1:
                 nc.sync.dma_start(out=roi_raw[:], in_=roi)
 
-        bias_rows = const.tile([P, HEAD_COLS], BF16)
-        nc.vector.memset(bias_rows[:], 0.0)
-        nc.scalar.dma_start(out=bias_rows[0:1, 0:CLS_COLS], in_=cls_b.unsqueeze(0))
-        nc.scalar.dma_start(out=bias_rows[0:1, CLS_COLS:HEAD_COLS], in_=bbox_b[P:].unsqueeze(0))
         convb_bf = const.tile([P, HALVES], BF16)
         nc.scalar.dma_start(out=convb_bf[:], in_=conv_b.rearrange("(q e) -> q e", e=HALVES))
 
@@ -275,25 +278,38 @@ def tile_classifiermodel_kernel(
         lin = const.tile([P, HEAD_COLS], F32)
 
         group_features(0)
+        quantise_features(0)
+        convolve(0)
+        transpose_features(1)
+        weight_tiles(0, 0)
+        weight_tiles(0, 1)
+        group_cls(0, 0)
+        group_hidden(0)
+        group_box(0, 0)
+        quantise_hidden(0)
         for g in range(CHUNKS):
-            weight_tiles(g, 0)
-            weight_tiles(g, 1)
-            quantise_features(g)
-            convolve(g)
-            group_cls(g, 0)
-            group_box(g, 0)
-            group_hidden(g)
-            if g + 1 < CHUNKS:
-                transpose_features(g + 1)
+            if g < last:
                 group_features(g + 1)
             if g > 0:
                 quantise_weights(g - 1, 1, all_columns)
                 head_pass(g - 1, 1, all_sums)
             if g < last:
-                group_box(g, 1)
+                quantise_features(g + 1)
+                convolve(g + 1)
+            if g > 0:
+                weight_tiles(g, 0)
+                weight_tiles(g, 1)
+                group_cls(g, 0)
+                group_box(g, 0)
+            if g + 2 < CHUNKS:
+                transpose_features(g + 2)
             group_cls(g, 1)
-            quantise_hidden(g)
+            if g < last:
+                group_box(g, 1)
+                group_hidden(g + 1)
             quantise_weights(g, 0, all_columns)
+            if g < last:
+                quantise_hidden(g + 1)
             head_pass(g, 0, all_sums)
             if g == 2:
                 nc.vector.tensor_scalar(
@@ -322,33 +338,39 @@ def tile_classifiermodel_kernel(
         quantise_weights(last, 1, ((B1, B2),))
         head_pass(last, 1, (shift_sums,))
 
+        clipped = const.tile([P, 2, P], F32)
+        grown = const.tile([P, 2, P], F32)
+        for i in range(2):
+            nc.vector.tensor_tensor(
+                out=lin[:, B2 + P * i : B2 + P * (i + 1)],
+                in0=acc_size[:, P * i : P * (i + 1)],
+                in1=bias_all[:, B2 + P * i : B2 + P * (i + 1)],
+                op=ALU.add,
+            )
+        for i in range(2):
+            nc.vector.tensor_scalar(
+                out=clipped[:, i, :],
+                in0=lin[:, B2 + P * i : B2 + P * (i + 1)],
+                scalar1=-10.0,
+                scalar2=10.0,
+                op0=ALU.max,
+                op1=ALU.min,
+            )
+            nc.scalar.activation(out=grown[:, i, :], in_=clipped[:, i, :], func=ACT.Exp)
         nc.vector.tensor_tensor(out=lin[:, 0:B1], in0=acc_cls[:], in1=bias_all[:, 0:B1], op=ALU.add)
-        nc.vector.tensor_tensor(
-            out=lin[:, B2:HEAD_COLS], in0=acc_size[:], in1=bias_all[:, B2:HEAD_COLS], op=ALU.add
-        )
+        nc.vector.tensor_tensor(out=lin[:, B1:B2], in0=acc_shift[:], in1=bias_all[:, B1:B2], op=ALU.add)
         margin = const.tile([P, P], F32)
         nc.vector.tensor_tensor(out=margin[:], in0=lin[:, P : 2 * P], in1=lin[:, 0:P], op=ALU.subtract)
-        clipped = const.tile([P, 2, P], F32)
-        nc.vector.tensor_scalar(
-            out=clipped[:].rearrange("b c n -> b (c n)"),
-            in0=lin[:, B2:HEAD_COLS],
-            scalar1=-10.0,
-            scalar2=10.0,
-            op0=ALU.max,
-            op1=ALU.min,
-        )
         squashed = const.tile([P, P], F32)
         nc.scalar.activation(out=squashed[:], in_=margin[:], func=ACT.Tanh, scale=0.5)
-        grown = const.tile([P, 2, P], F32)
-        nc.scalar.activation(out=grown[:], in_=clipped[:], func=ACT.Exp)
-        nc.vector.tensor_tensor(out=lin[:, B1:B2], in0=acc_shift[:], in1=bias_all[:, B1:B2], op=ALU.add)
+        shift = const.tile([P, P], F32)
+        nc.vector.tensor_tensor(out=shift[:], in0=lin[:, B1:B2], in1=r[:, 3, :], op=ALU.mult)
+        nc.vector.tensor_tensor(out=res[:, 2, :], in0=grown[:, 0, :], in1=r[:, 2, :], op=ALU.mult)
+        nc.vector.tensor_tensor(out=res[:, 0, :], in0=r[:, 0, :], in1=shift[:], op=ALU.subtract)
+        nc.vector.tensor_tensor(out=res[:, 3, :], in0=grown[:, 1, :], in1=r[:, 3, :], op=ALU.mult)
         nc.vector.tensor_scalar(
             out=res[:, 4, :], in0=squashed[:], scalar1=0.5, scalar2=0.5, op0=ALU.mult, op1=ALU.add
         )
-        shift = const.tile([P, P], F32)
-        nc.vector.tensor_tensor(out=shift[:], in0=lin[:, B1:B2], in1=r[:, 3, :], op=ALU.mult)
-        nc.vector.tensor_tensor(out=res[:, 2:4, :], in0=grown[:], in1=r[:, 2:4, :], op=ALU.mult)
-        nc.vector.tensor_tensor(out=res[:, 0, :], in0=r[:, 0, :], in1=shift[:], op=ALU.subtract)
         packed = const.tile([P, P, 5], F32)
         half = P // 2
         nc.vector.tensor_copy(

@@ -76,11 +76,6 @@ def tile_classifiermodel_kernel(
             box_rows = bbox_w[rows, P:].rearrange("(t q e) n -> q e t n", t=PACK, e=HALVES)
             nc.sync.dma_start(out=box_raw[(g, e)][:], in_=box_rows[:, e])
 
-        bias_rows = const.tile([P, HEAD_COLS], BF16)
-        nc.vector.memset(bias_rows[:], 0.0)
-        nc.sync.dma_start(out=bias_rows[0:1, 0:CLS_COLS], in_=cls_b.unsqueeze(0))
-        nc.sync.dma_start(out=bias_rows[0:1, CLS_COLS:HEAD_COLS], in_=bbox_b[P:].unsqueeze(0))
-
         feat_raw[0] = raw.tile([P, PACK, CHANNELS], BF16, name="feat_raw")
         load_positions(0, 0, 2)
         cw_raw = const.tile([P, PACK, HIDDEN], BF16)
@@ -89,6 +84,10 @@ def tile_classifiermodel_kernel(
             in_=conv_w.rearrange("(u q f) n -> q u f n", u=2, f=2),
         )
         load_positions(0, 2, PACK)
+        bias_rows = const.tile([P, HEAD_COLS], BF16)
+        nc.vector.memset(bias_rows[:], 0.0)
+        nc.sync.dma_start(out=bias_rows[0:1, 0:CLS_COLS], in_=cls_b.unsqueeze(0))
+        nc.sync.dma_start(out=bias_rows[0:1, CLS_COLS:HEAD_COLS], in_=bbox_b[P:].unsqueeze(0))
         roi_raw = const.tile([P, P, 4], BF16)
         for g in range(CHUNKS):
             load_cls(g)
@@ -98,8 +97,7 @@ def tile_classifiermodel_kernel(
             load_box(g, 1)
             if g + 2 < CHUNKS:
                 load_features(g + 2)
-            if g == 1:
-                nc.sync.dma_start(out=roi_raw[:], in_=roi)
+        nc.sync.dma_start(out=roi_raw[:], in_=roi)
 
         convb_bf = const.tile([P, HALVES], BF16)
         nc.scalar.dma_start(out=convb_bf[:], in_=conv_b.rearrange("(q e) -> q e", e=HALVES))
@@ -241,14 +239,6 @@ def tile_classifiermodel_kernel(
                     stop=(g == CHUNKS - 1 and e == HALVES - 1),
                 )
 
-        bias_all = const.tile([P, HEAD_COLS], F32)
-        for lo, hi in ((0, WIDE), (WIDE, HEAD_COLS)):
-            spread = psum_h.tile([P, WIDE], F32, name="hidden_ps")
-            nc.tensor.matmul(
-                out=spread[:, 0 : hi - lo], lhsT=ones[:], rhs=bias_rows[:, lo:hi], start=True, stop=True
-            )
-            nc.scalar.copy(out=bias_all[:, lo:hi], in_=spread[:, 0 : hi - lo])
-
         transpose_features(0)
 
         cw_grouped = const.tile([P, HIDDEN, PACK], BF16, align_bytes=64)
@@ -273,11 +263,18 @@ def tile_classifiermodel_kernel(
         size_sums = (B2, HEAD_COLS, acc_size)
         all_sums = (cls_sums, shift_sums, size_sums)
         last = CHUNKS - 1
-        r = const.tile([P, 4, P], F32)
         res = const.tile([P, 5, P], F32)
         lin = const.tile([P, HEAD_COLS], F32)
 
         group_features(0)
+        bias_all = const.tile([P, HEAD_COLS], F32)
+        for lo, hi in ((0, WIDE), (WIDE, HEAD_COLS)):
+            spread = psum_h.tile([P, WIDE], F32, name="hidden_ps")
+            nc.tensor.matmul(
+                out=spread[:, 0 : hi - lo], lhsT=ones[:], rhs=bias_rows[:, lo:hi], start=True, stop=True
+            )
+            nc.scalar.copy(out=bias_all[:, lo:hi], in_=spread[:, 0 : hi - lo])
+
         quantise_features(0)
         convolve(0)
         transpose_features(1)
@@ -311,15 +308,6 @@ def tile_classifiermodel_kernel(
             if g < last:
                 quantise_hidden(g + 1)
             head_pass(g, 0, all_sums)
-            if g == 2:
-                nc.vector.tensor_scalar(
-                    out=r[:],
-                    in0=roi_raw[:].rearrange("b n c -> b c n"),
-                    scalar1=STRIDE,
-                    scalar2=None,
-                    op0=ALU.mult,
-                )
-                nc.vector.tensor_copy(out=res[:, 1, :], in_=r[:, 1, :])
 
         grouped = w_grouped[(last, 1)]
 
@@ -331,6 +319,9 @@ def tile_classifiermodel_kernel(
 
         last_box(nc.vector.tensor_copy, P, BOX_COLS)
         last_box(nc.scalar.copy, 0, P)
+        nc.scalar.activation(
+            out=res[:, 0:4, :], in_=roi_raw[:].rearrange("b n c -> b c n"), func=ACT.Copy, scale=STRIDE
+        )
         quantise_weights(last, 1, ((0, B1),))
         head_pass(last, 1, (cls_sums,))
         quantise_weights(last, 1, ((B2, HEAD_COLS),))
@@ -364,18 +355,18 @@ def tile_classifiermodel_kernel(
         squashed = const.tile([P, P], F32)
         nc.scalar.activation(out=squashed[:], in_=margin[:], func=ACT.Tanh, scale=0.5)
         shift = const.tile([P, P], F32)
-        nc.vector.tensor_tensor(out=shift[:], in0=lin[:, B1:B2], in1=r[:, 3, :], op=ALU.mult)
-        nc.vector.tensor_tensor(out=res[:, 2, :], in0=grown[:, 0, :], in1=r[:, 2, :], op=ALU.mult)
-        nc.vector.tensor_tensor(out=res[:, 0, :], in0=r[:, 0, :], in1=shift[:], op=ALU.subtract)
-        nc.vector.tensor_tensor(out=res[:, 3, :], in0=grown[:, 1, :], in1=r[:, 3, :], op=ALU.mult)
+        nc.vector.tensor_tensor(out=shift[:], in0=lin[:, B1:B2], in1=res[:, 3, :], op=ALU.mult)
+        nc.vector.tensor_tensor(out=res[:, 2, :], in0=grown[:, 0, :], in1=res[:, 2, :], op=ALU.mult)
+        nc.vector.tensor_tensor(out=res[:, 0, :], in0=res[:, 0, :], in1=shift[:], op=ALU.subtract)
+        nc.vector.tensor_tensor(out=res[:, 3, :], in0=grown[:, 1, :], in1=res[:, 3, :], op=ALU.mult)
         nc.vector.tensor_scalar(
             out=res[:, 4, :], in0=squashed[:], scalar1=0.5, scalar2=0.5, op0=ALU.mult, op1=ALU.add
         )
         packed = const.tile([P, P, 5], F32)
-        half = P // 2
+        half = 5 * P // 8
         nc.vector.tensor_copy(
             out=packed[:, 0:half, :], in_=res[:, :, 0:half].rearrange("b c n -> b n c")
         )
         nc.scalar.copy(out=packed[:, half:P, :], in_=res[:, :, half:P].rearrange("b c n -> b n c"))
         nc.sync.dma_start(out=out[:, 0:half, :], in_=packed[:, 0:half, :])
-        nc.sync.dma_start(out=out[:, half:P, :], in_=packed[:, half:P, :])
+        nc.scalar.dma_start(out=out[:, half:P, :], in_=packed[:, half:P, :])

@@ -19,6 +19,7 @@ HIDDEN = 256
 CHUNKS = POSITIONS // PACK
 HALVES = HIDDEN // P
 CLS_COLS = 256
+MOVED_COLS = 192
 BOX_COLS = 384
 HEAD_COLS = CLS_COLS + BOX_COLS
 WIDE = 512
@@ -108,6 +109,8 @@ def tile_classifiermodel_kernel(
 
         ident = const.tile([P, P], F32)
         make_identity(nc, ident[:])
+        ident_bf = const.tile([P, P], BF16)
+        nc.gpsimd.tensor_copy(out=ident_bf[:], in_=ident[:])
         ones = const.tile([P, P], BF16)
         nc.vector.memset(ones[:], 1.0)
 
@@ -118,6 +121,7 @@ def tile_classifiermodel_kernel(
         feat_banks = {}
         feat_grouped = {}
         feat_codes = {}
+        cls_banks = {}
         hid_banks = {}
         hid_grouped = {}
         hid_codes = {}
@@ -193,10 +197,30 @@ def tile_classifiermodel_kernel(
             )
             hid_codes[g] = (codes, scales)
 
-        def group_cls(g, e):
+        def move_cls(g):
+            bank = psum_t.tile([P, 2, WIDE], BF16, name="feat_t")
+            part = MOVED_COLS // 2
+            for i in range(2):
+                nc.tensor.matmul(
+                    out=bank[:, i, 0 : PACK * part],
+                    lhsT=ident_bf[:],
+                    rhs=cls_raw[g][:, :, 1, part * i : part * (i + 1)].rearrange("q t n -> q n t"),
+                    start=True,
+                    stop=True,
+                )
+            cls_banks[g] = bank
+
+        def group_moved_cls(g):
+            part = MOVED_COLS // 2
             nc.scalar.copy(
-                out=w_grouped[(g, e)][:, 0:CLS_COLS, :].rearrange("q (c i) t -> q c t i", i=4),
-                in_=cls_raw[g][:, :, e, :].rearrange("q t (c i) -> q c t i", i=4),
+                out=w_grouped[(g, 1)][:, 0:MOVED_COLS, :].rearrange("q (i n) t -> q i (n t)", i=2),
+                in_=cls_banks[g][:, :, 0 : PACK * part],
+            )
+
+        def group_cls(g, e, lo):
+            nc.scalar.copy(
+                out=w_grouped[(g, e)][:, lo:CLS_COLS, :].rearrange("q (c i) t -> q c t i", i=4),
+                in_=cls_raw[g][:, :, e, lo:].rearrange("q t (c i) -> q c t i", i=4),
             )
 
         def group_box(g, e):
@@ -280,11 +304,12 @@ def tile_classifiermodel_kernel(
         transpose_features(1)
         weight_tiles(0, 0)
         weight_tiles(0, 1)
-        group_cls(0, 0)
+        group_cls(0, 0, 0)
         group_hidden(0)
         group_box(0, 0)
         quantise_hidden(0)
         for g in range(CHUNKS):
+            move_cls(g)
             if g < last:
                 group_features(g + 1)
             if g > 0:
@@ -296,11 +321,12 @@ def tile_classifiermodel_kernel(
             if g > 0:
                 weight_tiles(g, 0)
                 weight_tiles(g, 1)
-                group_cls(g, 0)
+                group_cls(g, 0, 0)
                 group_box(g, 0)
             if g + 2 < CHUNKS:
                 transpose_features(g + 2)
-            group_cls(g, 1)
+            group_moved_cls(g)
+            group_cls(g, 1, MOVED_COLS)
             if g < last:
                 group_box(g, 1)
                 group_hidden(g + 1)

from contextlib import ExitStack

import concourse.mybir as mybir
from concourse.masks import make_identity

F32 = mybir.dt.float32
BF16 = mybir.dt.bfloat16
U32 = mybir.dt.uint32
U8 = mybir.dt.uint8
FP8X4 = mybir.dt.float8_e4m3fn_x4
ACT = mybir.ActivationFunctionType
ALU = mybir.AluOpType

P = 128
PACK = 4
POSITIONS = 28
CHANNELS = 512
HIDDEN = 256
CHUNKS = POSITIONS // PACK
HALVES = HIDDEN // P
CLS_COLS = 256
MOVED_COLS = 192
BOX_COLS = 384
HEAD_COLS = CLS_COLS + BOX_COLS
WIDE = 512
B1 = CLS_COLS
B2 = CLS_COLS + P
STRIDE = 16.0

FLOPS = 2 * P * POSITIONS * CHANNELS * HIDDEN + 2 * P * POSITIONS * HIDDEN * HEAD_COLS
BYTES = (
    2 * (P * POSITIONS * CHANNELS + P * P * 4 + CHANNELS * HIDDEN + HIDDEN)
    + 2 * (POSITIONS * HIDDEN + 1) * HEAD_COLS
    + 4 * P * P * 5
)


def tile_classifiermodel_kernel(
    tc, features, roi, conv_w, conv_b, cls_w, cls_b, bbox_w, bbox_b, out
):
    nc = tc.nc
    with ExitStack() as ctx:
        const = ctx.enter_context(tc.tile_pool(name="const", bufs=1))
        raw = ctx.enter_context(tc.tile_pool(name="raw", bufs=CHUNKS))
        stage = ctx.enter_context(tc.tile_pool(name="stage", bufs=3))
        wstage = ctx.enter_context(tc.tile_pool(name="wstage", bufs=4))
        psum_t = ctx.enter_context(tc.psum_pool(name="psum_t", bufs=3))
        psum_h = ctx.enter_context(tc.psum_pool(name="psum_h", bufs=2))
        psum_acc = ctx.enter_context(tc.psum_pool(name="psum_acc", bufs=1))
        ctx.enter_context(tc.manual_schedule())

        feat_rows = features.rearrange("b h w c -> b (h w) c")
        feat_raw = {}
        cls_raw = {}
        box_raw = {}

        def load_features(g):
            feat_raw[g] = raw.tile([P, PACK, CHANNELS], BF16, name="feat_raw")
            load_positions(g, 0, PACK)

        def load_positions(g, lo, hi):
            nc.sync.dma_start(
                out=feat_raw[g][:, lo:hi, :], in_=feat_rows[:, PACK * g + lo : PACK * g + hi, :]
            )

        def load_cls(g):
            rows = slice(PACK * HIDDEN * g, PACK * HIDDEN * (g + 1))
            cls_raw[g] = raw.tile([P, PACK, HALVES, CLS_COLS], BF16, name="cls_raw")
            nc.sync.dma_start(
                out=cls_raw[g][:],
                in_=cls_w[rows, :].rearrange("(t q e) n -> q t e n", t=PACK, e=HALVES),
            )

        def load_box(g, e):
            rows = slice(PACK * HIDDEN * g, PACK * HIDDEN * (g + 1))
            box_raw[(g, e)] = raw.tile([P, PACK, BOX_COLS], BF16, name="box_raw", bufs=HALVES * CHUNKS)
            box_rows = bbox_w[rows, P:].rearrange("(t q e) n -> q e t n", t=PACK, e=HALVES)
            nc.sync.dma_start(out=box_raw[(g, e)][:], in_=box_rows[:, e])

        feat_raw[0] = raw.tile([P, PACK, CHANNELS], BF16, name="feat_raw")
        load_positions(0, 0, 2)
        cw_raw = const.tile([P, PACK, HIDDEN], BF16)
        nc.sync.dma_start(
            out=cw_raw[:].rearrange("q (u f) n -> q u f n", u=2),
            in_=conv_w.rearrange("(u q f) n -> q u f n", u=2, f=2),
        )
        load_positions(0, 2, PACK)
        bias_rows = const.tile([P, HEAD_COLS], BF16)
        nc.vector.memset(bias_rows[:], 0.0)
        nc.sync.dma_start(out=bias_rows[0:1, 0:CLS_COLS], in_=cls_b.unsqueeze(0))
        nc.sync.dma_start(out=bias_rows[0:1, CLS_COLS:HEAD_COLS], in_=bbox_b[P:].unsqueeze(0))
        roi_raw = const.tile([P, P, 4], BF16)
        for g in range(CHUNKS):
            load_cls(g)
            if g == 0:
                load_features(1)
            load_box(g, 0)
            load_box(g, 1)
            if g + 2 < CHUNKS:
                load_features(g + 2)
        nc.sync.dma_start(out=roi_raw[:], in_=roi)

        convb_bf = const.tile([P, HALVES], BF16)
        nc.scalar.dma_start(out=convb_bf[:], in_=conv_b.rearrange("(q e) -> q e", e=HALVES))

        warm = const.tile([P, 1], F32)
        nc.vector.memset(warm[:], 0.0)
        nc.scalar.activation(out=warm[:], in_=warm[:], func=ACT.Exp)

        ident = const.tile([P, P], F32)
        make_identity(nc, ident[:])
        ident_bf = const.tile([P, P], BF16)
        nc.gpsimd.tensor_copy(out=ident_bf[:], in_=ident[:])
        ones = const.tile([P, P], BF16)
        nc.vector.memset(ones[:], 1.0)

        acc_cls = psum_acc.tile([P, CLS_COLS], F32)
        acc_shift = psum_acc.tile([P, P], F32)
        acc_size = psum_acc.tile([P, 2 * P], F32)

        feat_banks = {}
        feat_grouped = {}
        feat_codes = {}
        cls_banks = {}
        hid_banks = {}
        hid_grouped = {}
        hid_codes = {}
        w_grouped = {}
        w_codes = {}

        def transpose_features(g):
            words = feat_raw[g][:].bitcast(F32)
            for pair in range(2):
                bank = psum_t.tile([P, 2, 2, P], F32, name="feat_t")
                for t in range(2):
                    for u in range(2):
                        nc.tensor.transpose(
                            bank[:, t, u, :], words[:, 2 * pair + t, P * u : P * (u + 1)], ident[:]
                        )
                feat_banks[(g, pair)] = bank

        def group_features(g):
            grouped = stage.tile([P, PACK * P, PACK], BF16, name="feat_grouped", align_bytes=64)
            grouped_words = grouped[:].bitcast(F32)
            for pair in range(2):
                nc.scalar.copy(
                    out=grouped_words[:, 2 * P * pair : 2 * P * (pair + 1), :].rearrange(
                        "q (t b) u -> q t b u", t=2
                    ),
                    in_=feat_banks[(g, pair)][:].rearrange("q t u b -> q t b u"),
                )
            feat_grouped[g] = grouped

        def quantise_features(g):
            codes = stage.tile([P, PACK * P], U32, name="feat_codes", align_bytes=64)
            scales = stage.tile([P, PACK * P], U8, name="feat_scales", align_bytes=64)
            nc.vector.quantize_mx(
                out=codes[:].bitcast(FP8X4),
                scales=scales[:],
                in_=feat_grouped[g][:].rearrange("q c k -> q (c k)"),
            )
            feat_codes[g] = (codes, scales)

        def convolve(g):
            codes, scales = feat_codes[g]
            for e in range(HALVES):
                hidden_ps = psum_h.tile([P, WIDE], F32, name="hidden_ps")
                nc.tensor.matmul_mx(
                    out=hidden_ps[:],
                    lhsT=cw_codes[:, P * e : P * (e + 1)].bitcast(FP8X4),
                    lhsT_scale=cw_scales[:, P * e : P * (e + 1)],
                    rhs=codes[:].bitcast(FP8X4),
                    rhs_scale=scales[:],
                    start=True,
                    stop=True,
                )
                hid_banks[(g, e)] = hidden_ps

        def group_hidden(g):
            grouped = stage.tile([P, HALVES, P, PACK], BF16, name="hid_grouped", align_bytes=64)
            for e in range(HALVES):
                nc.scalar.activation(
                    out=grouped[:, e],
                    in_=hid_banks[(g, e)][:].rearrange("q (t b) -> q b t", t=PACK),
                    func=ACT.Relu,
                    bias=convb[:, e : e + 1],
                )
            hid_grouped[g] = grouped

        def quantise_hidden(g):
            codes = stage.tile([P, HALVES, P], U32, name="hid_codes", align_bytes=64)
            scales = stage.tile([P, HALVES, P], U8, name="hid_scales", align_bytes=64)
            nc.vector.quantize_mx(
                out=codes[:].rearrange("q e b -> q (e b)").bitcast(FP8X4),
                scales=scales[:].rearrange("q e b -> q (e b)"),
                in_=hid_grouped[g][:].rearrange("q e b t -> q (e b t)"),
            )
            hid_codes[g] = (codes, scales)

        def move_cls(g):
            bank = psum_t.tile([P, 2, WIDE], BF16, name="feat_t")
            part = MOVED_COLS // 2
            for i in range(2):
                nc.tensor.matmul(
                    out=bank[:, i, 0 : PACK * part],
                    lhsT=ident_bf[:],
                    rhs=cls_raw[g][:, :, 1, part * i : part * (i + 1)].rearrange("q t n -> q n t"),
                    start=True,
                    stop=True,
                )
            cls_banks[g] = bank

        def group_moved_cls(g):
            part = MOVED_COLS // 2
            nc.scalar.copy(
                out=w_grouped[(g, 1)][:, 0:MOVED_COLS, :].rearrange("q (i n) t -> q i (n t)", i=2),
                in_=cls_banks[g][:, :, 0 : PACK * part],
            )

        def group_cls(g, e, lo):
            nc.scalar.copy(
                out=w_grouped[(g, e)][:, lo:CLS_COLS, :].rearrange("q (c i) t -> q c t i", i=4),
                in_=cls_raw[g][:, :, e, lo:].rearrange("q t (c i) -> q c t i", i=4),
            )

        def group_box(g, e):
            nc.vector.tensor_copy(
                out=w_grouped[(g, e)][:, CLS_COLS:HEAD_COLS, :].rearrange(
                    "q (c i) t -> q c t i", i=4
                ),
                in_=box_raw[(g, e)][:].rearrange("q t (c i) -> q c t i", i=4),
            )

        def weight_tiles(g, e):
            w_grouped[(g, e)] = wstage.tile(
                [P, HEAD_COLS, PACK], BF16, name="w_grouped", align_bytes=64
            )
            codes = wstage.tile([P, HEAD_COLS], U32, name="w_codes", align_bytes=64)
            scales = wstage.tile([P, HEAD_COLS], U8, name="w_scales", align_bytes=64)
            w_codes[(g, e)] = (codes, scales)

        def quantise_weights(g, e, columns):
            flat_in = w_grouped[(g, e)][:].rearrange("q n t -> q (n t)")
            codes, scales = w_codes[(g, e)]
            for lo, hi in columns:
                nc.vector.quantize_mx(
                    out=codes[:, lo:hi].bitcast(FP8X4),
                    scales=scales[:, lo:hi],
                    in_=flat_in[:, PACK * lo : PACK * hi],
                )

        def head_pass(g, e, sums):
            codes, scales = w_codes[(g, e)]
            h_codes, h_scales = hid_codes[g]
            for lo, hi, acc in sums:
                nc.tensor.matmul_mx(
                    out=acc[:],
                    lhsT=h_codes[:, e, :].bitcast(FP8X4),
                    lhsT_scale=h_scales[:, e, :],
                    rhs=codes[:, lo:hi].bitcast(FP8X4),
                    rhs_scale=scales[:, lo:hi],
                    start=(g == 0 and e == 0),
                    stop=(g == CHUNKS - 1 and e == HALVES - 1),
                )

        transpose_features(0)

        cw_grouped = const.tile([P, HIDDEN, PACK], BF16, align_bytes=64)
        for e in range(HALVES):
            nc.vector.tensor_copy(
                out=cw_grouped[:, P * e : P * (e + 1), :],
                in_=cw_raw[:].rearrange("q k (m e) -> q e m k", e=HALVES)[:, e],
            )
        convb = const.tile([P, HALVES], F32)
        nc.vector.tensor_copy(out=convb[:], in_=convb_bf[:])
        cw_codes = const.tile([P, HIDDEN], U32, align_bytes=64)
        cw_scales = const.tile([P, HIDDEN], U8, align_bytes=64)
        nc.vector.quantize_mx(
            out=cw_codes[:].bitcast(FP8X4),
            scales=cw_scales[:],
            in_=cw_grouped[:].rearrange("q n k -> q (n k)"),
        )

        all_columns = ((0, WIDE), (WIDE, HEAD_COLS))
        cls_sums = (0, B1, acc_cls)
        shift_sums = (B1, B2, acc_shift)
        size_sums = (B2, HEAD_COLS, acc_size)
        all_sums = (cls_sums, shift_sums, size_sums)
        last = CHUNKS - 1
        res = const.tile([P, 5, P], F32)
        lin = const.tile([P, HEAD_COLS], F32)

        group_features(0)
        bias_all = const.tile([P, HEAD_COLS], F32)
        for lo, hi in ((0, WIDE), (WIDE, HEAD_COLS)):
            spread = psum_h.tile([P, WIDE], F32, name="hidden_ps")
            nc.tensor.matmul(
                out=spread[:, 0 : hi - lo], lhsT=ones[:], rhs=bias_rows[:, lo:hi], start=True, stop=True
            )
            nc.scalar.copy(out=bias_all[:, lo:hi], in_=spread[:, 0 : hi - lo])

        quantise_features(0)
        convolve(0)
        transpose_features(1)
        weight_tiles(0, 0)
        weight_tiles(0, 1)
        group_cls(0, 0, 0)
        group_hidden(0)
        group_box(0, 0)
        quantise_hidden(0)
        for g in range(CHUNKS):
            move_cls(g)
            if g < last:
                group_features(g + 1)
            if g > 0:
                quantise_weights(g - 1, 1, all_columns)
                head_pass(g - 1, 1, all_sums)
            if g < last:
                quantise_features(g + 1)
                convolve(g + 1)
            if g > 0:
                weight_tiles(g, 0)
                weight_tiles(g, 1)
                group_cls(g, 0, 0)
                group_box(g, 0)
            if g + 2 < CHUNKS:
                transpose_features(g + 2)
            group_moved_cls(g)
            group_cls(g, 1, MOVED_COLS)
            if g < last:
                group_box(g, 1)
                group_hidden(g + 1)
            quantise_weights(g, 0, all_columns)
            if g < last:
                quantise_hidden(g + 1)
            head_pass(g, 0, all_sums)

        grouped = w_grouped[(last, 1)]

        def last_box(copy, lo, hi):
            copy(
                out=grouped[:, CLS_COLS + lo : CLS_COLS + hi, :].rearrange("q (c i) t -> q c t i", i=4),
                in_=box_raw[(last, 1)][:, :, lo:hi].rearrange("q t (c i) -> q c t i", i=4),
            )

        last_box(nc.vector.tensor_copy, P, BOX_COLS)
        last_box(nc.scalar.copy, 0, P)
        nc.scalar.activation(
            out=res[:, 0:4, :], in_=roi_raw[:].rearrange("b n c -> b c n"), func=ACT.Copy, scale=STRIDE
        )
        quantise_weights(last, 1, ((0, B1),))
        head_pass(last, 1, (cls_sums,))
        quantise_weights(last, 1, ((B2, HEAD_COLS),))
        head_pass(last, 1, (size_sums,))
        quantise_weights(last, 1, ((B1, B2),))
        head_pass(last, 1, (shift_sums,))

        clipped = const.tile([P, 2, P], F32)
        grown = const.tile([P, 2, P], F32)
        for i in range(2):
            nc.vector.tensor_tensor(
                out=lin[:, B2 + P * i : B2 + P * (i + 1)],
                in0=acc_size[:, P * i : P * (i + 1)],
                in1=bias_all[:, B2 + P * i : B2 + P * (i + 1)],
                op=ALU.add,
            )
        for i in range(2):
            nc.vector.tensor_scalar(
                out=clipped[:, i, :],
                in0=lin[:, B2 + P * i : B2 + P * (i + 1)],
                scalar1=-10.0,
                scalar2=10.0,
                op0=ALU.max,
                op1=ALU.min,
            )
            nc.scalar.activation(out=grown[:, i, :], in_=clipped[:, i, :], func=ACT.Exp)
        nc.vector.tensor_tensor(out=lin[:, 0:B1], in0=acc_cls[:], in1=bias_all[:, 0:B1], op=ALU.add)
        nc.vector.tensor_tensor(out=lin[:, B1:B2], in0=acc_shift[:], in1=bias_all[:, B1:B2], op=ALU.add)
        margin = const.tile([P, P], F32)
        nc.vector.tensor_tensor(out=margin[:], in0=lin[:, P : 2 * P], in1=lin[:, 0:P], op=ALU.subtract)
        squashed = const.tile([P, P], F32)
        nc.scalar.activation(out=squashed[:], in_=margin[:], func=ACT.Tanh, scale=0.5)
        shift = const.tile([P, P], F32)
        nc.vector.tensor_tensor(out=shift[:], in0=lin[:, B1:B2], in1=res[:, 3, :], op=ALU.mult)
        nc.vector.tensor_tensor(out=res[:, 2, :], in0=grown[:, 0, :], in1=res[:, 2, :], op=ALU.mult)
        nc.vector.tensor_tensor(out=res[:, 0, :], in0=res[:, 0, :], in1=shift[:], op=ALU.subtract)
        nc.vector.tensor_tensor(out=res[:, 3, :], in0=grown[:, 1, :], in1=res[:, 3, :], op=ALU.mult)
        nc.vector.tensor_scalar(
            out=res[:, 4, :], in0=squashed[:], scalar1=0.5, scalar2=0.5, op0=ALU.mult, op1=ALU.add
        )
        packed = const.tile([P, P, 5], F32)
        half = 5 * P // 8
        nc.vector.tensor_copy(
            out=packed[:, 0:half, :], in_=res[:, :, 0:half].rearrange("b c n -> b n c")
        )
        nc.scalar.copy(out=packed[:, half:P, :], in_=res[:, :, half:P].rearrange("b c n -> b n c"))
        nc.sync.dma_start(out=out[:, 0:half, :], in_=packed[:, 0:half, :])
        nc.scalar.dma_start(out=out[:, half:P, :], in_=packed[:, half:P, :])
